import numpy as np
import ml_dtypes


def mxq(x, axis, fmt="e4m3"):
    dtype, down = {"e4m3": (ml_dtypes.float8_e4m3fn, 7), "e5m2": (ml_dtypes.float8_e5m2, 14)}[fmt]
    v = np.moveaxis(np.asarray(x, np.float32).astype(ml_dtypes.bfloat16).astype(np.float64), axis, -1)
    blocks = v.reshape(v.shape[:-1] + (-1, 32))
    amax = np.abs(blocks).max(-1, keepdims=True)
    byte = np.maximum(np.where(amax > 0, np.frexp(amax)[1] - 1 + 127, 0) - down, 1)
    scale = np.exp2(byte - 127.0)
    codes = (blocks / scale).astype(np.float32).astype(dtype).astype(np.float64)
    return np.moveaxis((codes * scale).reshape(v.shape), -1, axis)


WIDE = False


def mx_kscale(k):
    if not WIDE:
        return np.ones(k)
    levels = np.array([10, -10, 5, -5, 0])
    a = np.random.permutation(np.resize(levels, k // 512 * 4)).reshape(k // 512, 4)
    idx = np.arange(k)
    return np.exp2(a[idx // 512, idx % 128 // 32])


BF16 = ml_dtypes.bfloat16


def bf(x):
    return np.asarray(x, np.float32).astype(BF16)


def f64(x):
    return np.asarray(x).astype(np.float64)


BS, L, D, E, H = 16, 256, 512, 512, 2
LAMBDA_ATTN = 10.0


def l2norm(x, eps=1e-12):
    n = np.sqrt(np.sum(x * x, axis=-1, keepdims=True))
    return x / np.maximum(n, eps)


def softmax(x, axis):
    e = np.exp(x - x.max(axis=axis, keepdims=True))
    return e / e.sum(axis=axis, keepdims=True)


def setup_inputs():
    s = mx_kscale(D)
    g1 = np.exp2(np.random.uniform(-1.0, 1.0, (BS, 1, L)))
    g2 = np.exp2(np.random.uniform(-1.0, 1.0, (BS, 1, L)))
    return {"img1": bf(np.random.standard_normal((BS, D, L)) * g1 * s[None, :, None]),
            "img2": bf(np.random.standard_normal((BS, D, L)) * g2 * s[None, :, None]),
            "W": bf(np.random.standard_normal((H, D, E)) / np.sqrt(D) / s[None, :, None]),
            "b": bf(np.random.standard_normal((H, E)) * 0.5)}


def reference(img1, img2, W, b):
    x1 = np.swapaxes(mxq(f64(img1), 1, "e4m3"), 1, 2)
    x2 = np.swapaxes(mxq(f64(img2), 1, "e4m3"), 1, 2)
    Wf = mxq(f64(W), 1, "e4m3").transpose(1, 0, 2).reshape(D, H * E)
    bb = f64(b)[:, None, None, :]
    q1 = (x1 @ Wf).reshape(BS, L, H, E).transpose(2, 0, 1, 3) + bb
    q2 = (x2 @ Wf).reshape(BS, L, H, E).transpose(2, 0, 1, 3) + bb
    n1 = l2norm(q1)
    n2 = l2norm(q2)
    rel = (mxq(n1, 3, "e4m3") @ mxq(n2, 3, "e4m3").transpose(0, 1, 3, 2)) * LAMBDA_ATTN
    row_attn = softmax(rel, 3)
    col_attn = softmax(rel, 2)
    sim12 = row_attn.sum(axis=2)
    sim21 = col_attn.sum(axis=3)
    sim12 = sim12 / (sim12.sum(axis=-1, keepdims=True) + 1e-8)
    sim21 = sim21 / (sim21.sum(axis=-1, keepdims=True) + 1e-8)
    return np.stack([sim21, sim12], axis=0)

@@ -1,0 +1,350 @@
+from contextlib import ExitStack
+
+import concourse.mybir as mybir
+from concourse.masks import make_identity
+
+FP8X4 = mybir.dt.float8_e4m3fn_x4
+BF16 = mybir.dt.bfloat16
+F32 = mybir.dt.float32
+U32 = mybir.dt.uint32
+U8 = mybir.dt.uint8
+ALU = mybir.AluOpType
+ACT = mybir.ActivationFunctionType
+
+P = 128
+BS, L, D, E, H = 16, 256, 512, 512, 2
+PACK = 4
+NPOS = 2 * L
+UNITS = BS * H
+LAMBDA = 10.0
+FLOPS = 2 * (2 * BS * L) * D * (H * E) + 2 * H * BS * L * L * E
+W2_SLOTS = 4
+RAW_BUFS = 4
+
+
+def tile_oaclipv3_t_kernel(tc, img1, img2, W, b, out):
+    nc = tc.nc
+    with ExitStack() as ctx:
+        const = ctx.enter_context(tc.tile_pool(name="const", bufs=1))
+        rawp = ctx.enter_context(tc.tile_pool(name="rawp", bufs=RAW_BUFS))
+        xgp = ctx.enter_context(tc.tile_pool(name="xgp", bufs=2))
+        xcp = ctx.enter_context(tc.tile_pool(name="xcp", bufs=3))
+        qbp = ctx.enter_context(tc.tile_pool(name="qbp", bufs=4))
+        junkp = ctx.enter_context(tc.tile_pool(name="junkp", bufs=2))
+        ngp = ctx.enter_context(tc.tile_pool(name="ngp", bufs=3))
+        ncp = ctx.enter_context(tc.tile_pool(name="ncp", bufs=3))
+        ep = ctx.enter_context(tc.tile_pool(name="ep", bufs=3))
+        smallp = ctx.enter_context(tc.tile_pool(name="smallp", bufs=4))
+        psq = ctx.enter_context(tc.psum_pool(name="psq", bufs=3))
+        pstr = ctx.enter_context(tc.psum_pool(name="pstr", bufs=2))
+        psr = ctx.enter_context(tc.psum_pool(name="psr", bufs=1))
+        psrel = ctx.enter_context(tc.psum_pool(name="psrel", bufs=1))
+        psfin = ctx.enter_context(tc.psum_pool(name="psfin", bufs=1))
+        ctx.enter_context(tc.manual_schedule())
+
+        w_raw = const.tile([P, H, PACK, E], BF16)
+        b_raw = const.tile([P, H, PACK], BF16)
+        ident = const.tile([P, P], F32)
+        ones = const.tile([P, P], F32)
+        mhalf = const.tile([P, 4], F32)
+        w2 = const.tile([P, W2_SLOTS, 2, 2], F32)
+        res = const.tile([P, 128], F32)
+        b32 = const.tile([P, H * PACK], F32)
+        w_grp = const.tile([P, H, PACK, P, PACK], BF16, align_bytes=64)
+        w_cod = const.tile([P, H * PACK * P], U32, align_bytes=64)
+        w_scl = const.tile([P, H * PACK * P], U8, align_bytes=64)
+
+        raws, xgs, xcs, xss = {}, {}, {}, {}
+        qs, qbs, trs, nrms, rns, rbcs, ngs, ncods, nscls = {}, {}, {}, {}, {}, {}, {}, {}, {}
+        rels, exs, rss, fins, rcs = {}, {}, {}, {}, {}
+
+        def load_w(h):
+            nc.sync.dma_start(out=w_raw[:, h], in_=W[h].rearrange("(p j) e -> p j e", j=PACK))
+
+        def load_img(i):
+            raw = rawp.tile([P, 2, PACK, L], BF16)
+            nc.sync.dma_start(out=raw[:, 0], in_=img1[i].rearrange("(p j) l -> p j l", j=PACK))
+            nc.sync.dma_start(out=raw[:, 1], in_=img2[i].rearrange("(p j) l -> p j l", j=PACK))
+            raws[i] = raw
+
+        def quant_w(h):
+            cols = slice(h * PACK * P, (h + 1) * PACK * P)
+            nc.vector.quantize_mx(
+                out=w_cod[:, cols].bitcast(FP8X4),
+                scales=w_scl[:, cols],
+                in_=w_grp[:, h].rearrange("p t m j -> p (t m j)"),
+            )
+
+        def regroup_img(i):
+            xg = xgp.tile([P, 2, L, PACK], BF16, align_bytes=64)
+            for s in range(2):
+                nc.vector.tensor_copy(
+                    out=xg[:, s].rearrange("p (c r) j -> p c j r", r=4),
+                    in_=raws[i][:, s].rearrange("p j (c r) -> p c j r", r=4),
+                )
+            xgs[i] = xg
+
+        def quant_img(i):
+            xc = xcp.tile([P, NPOS], U32, align_bytes=64)
+            xs = xcp.tile([P, NPOS], U8, align_bytes=64)
+            nc.vector.quantize_mx(
+                out=xc[:].bitcast(FP8X4),
+                scales=xs[:],
+                in_=xgs[i][:].rearrange("p s l j -> p (s l j)"),
+            )
+            xcs[i] = xc
+            xss[i] = xs
+
+        def project(u, t):
+            i, h = divmod(u, H)
+            q = psq.tile([P, NPOS], F32)
+            wcols = slice((h * PACK + t) * P, (h * PACK + t + 1) * P)
+            nc.tensor.matmul_mx(
+                out=q[:],
+                lhsT=w_cod[:, wcols].bitcast(FP8X4),
+                lhsT_scale=w_scl[:, wcols],
+                rhs=xcs[i][:].bitcast(FP8X4),
+                rhs_scale=xss[i][:],
+                start=True,
+                stop=True,
+            )
+            qs[(u, t)] = q
+
+        def add_bias(u, t):
+            h = u % H
+            if t == 0:
+                qb = qbp.tile([P, PACK, NPOS], F32)
+                qbs[u] = qb
+            nc.scalar.activation(
+                out=qbs[u][:, t, :],
+                in_=qs[(u, t)][:],
+                func=ACT.Identity,
+                bias=b32[:, h * PACK + t : h * PACK + t + 1],
+                scale=1.0,
+            )
+
+        def flip(u, c):
+            tr = pstr.tile([P, PACK * P], F32)
+            for t in range(PACK):
+                nc.tensor.transpose(
+                    out=tr[:, t * P : (t + 1) * P],
+                    in_=qbs[u][:, t, c * P : (c + 1) * P],
+                    identity=ident[:],
+                )
+            trs[(u, c)] = tr
+
+        def square_sum(u, c):
+            if c == 0:
+                nrm2 = smallp.tile([P, 4], F32)
+                nrms[u] = nrm2
+            sqj = junkp.tile([P, PACK * P], BF16)
+            nc.scalar.activation(
+                out=sqj[:], in_=trs[(u, c)][:], func=ACT.Square, accum_out=nrms[u][:, c : c + 1]
+            )
+
+        def inv_norm(u):
+            ncl = smallp.tile([P, 4], F32)
+            nc.gpsimd.tensor_scalar(
+                out=ncl[:], in0=nrms[u][:], scalar1=1e-24, scalar2=None, op0=ALU.max
+            )
+            rn = smallp.tile([P, 4], F32)
+            nc.gpsimd.tensor_tensor(out=rn[:], in0=ncl[:], in1=mhalf[:], op=ALU.pow)
+            rns[u] = rn
+
+        def spread_inv_norm(u):
+            rbc = psr.tile([P, NPOS], F32)
+            for c in range(4):
+                nc.tensor.transpose(
+                    out=rbc[:, c * P : (c + 1) * P],
+                    in_=rns[u][:, c : c + 1].to_broadcast([P, P]),
+                    identity=ident[:],
+                )
+            rbcs[u] = rbc
+
+        def normalise(u):
+            ng = ngp.tile([P, NPOS, PACK], BF16, align_bytes=64)
+            nc.vector.tensor_tensor(
+                out=ng[:],
+                in0=qbs[u][:].rearrange("p t c -> p c t"),
+                in1=rbcs[u][:].unsqueeze(2).to_broadcast([P, NPOS, PACK]),
+                op=ALU.mult,
+            )
+            ngs[u] = ng
+
+        def quant_n(u):
+            ncod = ncp.tile([P, NPOS], U32, align_bytes=64)
+            nscl = ncp.tile([P, NPOS], U8, align_bytes=64)
+            nc.vector.quantize_mx(
+                out=ncod[:].bitcast(FP8X4),
+                scales=nscl[:],
+                in_=ngs[u][:].rearrange("p c t -> p (c t)"),
+            )
+            ncods[u] = ncod
+            nscls[u] = nscl
+
+        def cosines(u):
+            rel = psrel.tile([P, 2, L], F32)
+            for lb in range(2):
+                nc.tensor.matmul_mx(
+                    out=rel[:, lb, :],
+                    lhsT=ncods[u][:, lb * P : (lb + 1) * P].bitcast(FP8X4),
+                    lhsT_scale=nscls[u][:, lb * P : (lb + 1) * P],
+                    rhs=ncods[u][:, L : 2 * L].bitcast(FP8X4),
+                    rhs_scale=nscls[u][:, L : 2 * L],
+                    start=True,
+                    stop=True,
+                )
+            rels[u] = rel
+
+        def exponent(u):
+            ex = ep.tile([P, 2, L], F32)
+            rs = smallp.tile([P, 2], F32)
+            for lb in range(2):
+                nc.scalar.activation(
+                    out=ex[:, lb, :],
+                    in_=rels[u][:, lb, :],
+                    func=ACT.Exp,
+                    bias=-LAMBDA,
+                    scale=LAMBDA,
+                    accum_out=rs[:, lb : lb + 1],
+                )
+            exs[u] = ex
+            rss[u] = rs
+
+        def inv_rowsum(u):
+            nc.vector.reciprocal(out=w2[:, u % W2_SLOTS, :, 1], in_=rss[u][:])
+
+        def column_sums(u):
+            fin = psfin.tile([P, 512], F32)
+            for mb in range(2):
+                for lb in range(2):
+                    nc.tensor.matmul(
+                        out=fin[:, L + 2 * mb : L + 2 * mb + 2],
+                        lhsT=exs[u][:, lb, mb * P : (mb + 1) * P],
+                        rhs=w2[:, u % W2_SLOTS, lb, :],
+                        start=(lb == 0),
+                        stop=(lb == 1),
+                    )
+            fins[u] = fin
+
+        def inv_colsum(u):
+            i, h = divmod(u, H)
+            cs = fins[u][:, L : L + 4].rearrange("p (m k) -> p m k", k=2)
+            rc = smallp.tile([P, 2], F32)
+            nc.vector.reciprocal(out=rc[:], in_=cs[:, :, 0])
+            col12 = ((2 + h) * BS + i) * 2
+            nc.vector.tensor_copy(out=res[:, col12 : col12 + 2], in_=cs[:, :, 1])
+            rcs[u] = rc
+
+        def spread_inv_colsum(u):
+            for mb in range(2):
+                nc.tensor.transpose(
+                    out=fins[u][:, mb * P : (mb + 1) * P],
+                    in_=rcs[u][:, mb : mb + 1].to_broadcast([P, P]),
+                    identity=ident[:],
+                )
+
+        def row_of_col_attn(u):
+            i, h = divmod(u, H)
+            col21 = (h * BS + i) * 2
+            for lb in range(2):
+                pj = junkp.tile([P, L], F32)
+                nc.vector.scalar_tensor_tensor(
+                    out=pj[:],
+                    in0=exs[u][:, lb, :],
+                    scalar=1.0,
+                    in1=fins[u][:, 0:L],
+                    op0=ALU.mult,
+                    op1=ALU.mult,
+                    accum_out=res[:, col21 + lb : col21 + lb + 1],
+                )
+
+        def live(u):
+            return 0 <= u < UNITS
+
+        load_w(0)
+        load_img(0)
+        load_w(1)
+        for i in range(1, RAW_BUFS):
+            load_img(i)
+        with nc.allow_non_contiguous_dma(reason="bias: four neighbouring values to a partition"):
+            nc.scalar.dma_start(out=b_raw[:], in_=b.rearrange("h (m t) -> m h t", t=PACK))
+        make_identity(nc, ident[:])
+        nc.vector.memset(mhalf[:], -0.5)
+        nc.vector.memset(w2[:], 1.0)
+        nc.vector.memset(ones[:], 1.0)
+        nc.vector.tensor_copy(
+            out=w_grp[:, 0], in_=w_raw[:, 0].rearrange("p j (m t) -> p t m j", t=PACK)
+        )
+        nc.scalar.copy(out=w_grp[:, 1], in_=w_raw[:, 1].rearrange("p j (m t) -> p t m j", t=PACK))
+        regroup_img(0)
+        quant_w(0)
+        quant_img(0)
+        nc.vector.tensor_copy(out=b32[:], in_=b_raw[:].rearrange("p h t -> p (h t)"))
+        quant_w(1)
+        for t in range(3):
+            project(0, t)
+
+        for k in range(UNITS + 4):
+            if live(k - 2):
+                cosines(k - 2)
+            if live(k - 3):
+                inv_rowsum(k - 3)
+                column_sums(k - 3)
+            if live(k):
+                add_bias(k, 0)
+                add_bias(k, 1)
+                project(k, 3)
+                add_bias(k, 2)
+                add_bias(k, 3)
+            if k % 2 == 0 and k // 2 + 1 < BS:
+                regroup_img(k // 2 + 1)
+                if k // 2 + 1 + RAW_BUFS - 1 < BS:
+                    load_img(k // 2 + RAW_BUFS)
+            if live(k - 3):
+                inv_colsum(k - 3)
+                spread_inv_colsum(k - 3)
+            if k % 2 == 1 and (k + 1) // 2 < BS:
+                quant_img((k + 1) // 2)
+            if live(k - 3):
+                row_of_col_attn(k - 3)
+            if live(k - 2):
+                exponent(k - 2)
+            if live(k - 1):
+                spread_inv_norm(k - 1)
+                normalise(k - 1)
+                quant_n(k - 1)
+            if live(k):
+                flip(k, 0)
+                flip(k, 1)
+                square_sum(k, 0)
+                flip(k, 2)
+                square_sum(k, 1)
+                flip(k, 3)
+                square_sum(k, 2)
+                square_sum(k, 3)
+                inv_norm(k)
+            if live(k + 1):
+                for t in range(3):
+                    project(k + 1, t)
+
+        resv = res[:].rearrange("p (c f) -> p c f", f=2)
+        tot = psfin.tile([P, 512], F32, tag="fin")
+        nc.tensor.matmul(out=tot[:, 0:64], lhsT=ones[:], rhs=resv[:, :, 0], start=True, stop=False)
+        nc.tensor.matmul(out=tot[:, 0:64], lhsT=ones[:], rhs=resv[:, :, 1], start=False, stop=True)
+        den = const.tile([P, 64], F32)
+        nc.vector.tensor_scalar(out=den[:], in0=tot[:, 0:64], scalar1=1e-8, scalar2=None, op0=ALU.add)
+        rden = const.tile([P, 64], F32)
+        nc.vector.reciprocal(out=rden[:], in_=den[:])
+        resn = const.tile([P, 128], F32)
+        nc.vector.tensor_tensor(
+            out=resn[:].rearrange("p (c f) -> p c f", f=2),
+            in0=resv,
+            in1=rden[:].unsqueeze(2).to_broadcast([P, 64, 2]),
+            op=ALU.mult,
+        )
+        rt = pstr.tile([P, PACK * P], F32, tag="tr")
+        nc.tensor.transpose(out=rt[:, 0:P], in_=resn[:], identity=ident[:])
+        o_sb = const.tile([P, P], F32)
+        nc.vector.tensor_copy(out=o_sb[:], in_=rt[:, 0:P])
+        nc.sync.dma_start(out=out.rearrange("w h i (f p) -> (w h i f) p", p=P), in_=o_sb[:])

@@ -29,16 +29,14 @@ def tile_oaclipv3_t_kernel(tc, img1, img2, W, b, out):
         rawp = ctx.enter_context(tc.tile_pool(name="rawp", bufs=RAW_BUFS))
         xgp = ctx.enter_context(tc.tile_pool(name="xgp", bufs=2))
         xcp = ctx.enter_context(tc.tile_pool(name="xcp", bufs=3))
-        qbp = ctx.enter_context(tc.tile_pool(name="qbp", bufs=4))
+        qbp = ctx.enter_context(tc.tile_pool(name="qbp", bufs=5))
         junkp = ctx.enter_context(tc.tile_pool(name="junkp", bufs=2))
         ngp = ctx.enter_context(tc.tile_pool(name="ngp", bufs=3))
         ncp = ctx.enter_context(tc.tile_pool(name="ncp", bufs=3))
-        ep = ctx.enter_context(tc.tile_pool(name="ep", bufs=3))
+        ep = ctx.enter_context(tc.tile_pool(name="ep", bufs=4))
         smallp = ctx.enter_context(tc.tile_pool(name="smallp", bufs=4))
-        psq = ctx.enter_context(tc.psum_pool(name="psq", bufs=3))
-        pstr = ctx.enter_context(tc.psum_pool(name="pstr", bufs=2))
+        ring = ctx.enter_context(tc.psum_pool(name="ring", bufs=6))
         psr = ctx.enter_context(tc.psum_pool(name="psr", bufs=1))
-        psrel = ctx.enter_context(tc.psum_pool(name="psrel", bufs=1))
         psfin = ctx.enter_context(tc.psum_pool(name="psfin", bufs=1))
         ctx.enter_context(tc.manual_schedule())
 
@@ -97,7 +95,7 @@ def tile_oaclipv3_t_kernel(tc, img1, img2, W, b, out):
 
         def project(u, t):
             i, h = divmod(u, H)
-            q = psq.tile([P, NPOS], F32)
+            q = ring.tile([P, NPOS], F32, tag="feed")
             wcols = slice((h * PACK + t) * P, (h * PACK + t + 1) * P)
             nc.tensor.matmul_mx(
                 out=q[:],
@@ -124,7 +122,7 @@ def tile_oaclipv3_t_kernel(tc, img1, img2, W, b, out):
             )
 
         def flip(u, c):
-            tr = pstr.tile([P, PACK * P], F32)
+            tr = ring.tile([P, PACK * P], F32, tag="feed")
             for t in range(PACK):
                 nc.tensor.transpose(
                     out=tr[:, t * P : (t + 1) * P],
@@ -183,7 +181,7 @@ def tile_oaclipv3_t_kernel(tc, img1, img2, W, b, out):
             nscls[u] = nscl
 
         def cosines(u):
-            rel = psrel.tile([P, 2, L], F32)
+            rel = ring.tile([P, 2, L], F32, tag="feed")
             for lb in range(2):
                 nc.tensor.matmul_mx(
                     out=rel[:, lb, :],
@@ -278,55 +276,69 @@ def tile_oaclipv3_t_kernel(tc, img1, img2, W, b, out):
         )
         nc.scalar.copy(out=w_grp[:, 1], in_=w_raw[:, 1].rearrange("p j (m t) -> p t m j", t=PACK))
         regroup_img(0)
+        load_img(RAW_BUFS)
         quant_w(0)
         quant_img(0)
         nc.vector.tensor_copy(out=b32[:], in_=b_raw[:].rearrange("p h t -> p (h t)"))
+        regroup_img(1)
+        load_img(RAW_BUFS + 1)
         quant_w(1)
-        for t in range(3):
-            project(0, t)
 
-        for k in range(UNITS + 4):
-            if live(k - 2):
-                cosines(k - 2)
-            if live(k - 3):
-                inv_rowsum(k - 3)
-                column_sums(k - 3)
-            if live(k):
-                add_bias(k, 0)
-                add_bias(k, 1)
-                project(k, 3)
-                add_bias(k, 2)
-                add_bias(k, 3)
-            if k % 2 == 0 and k // 2 + 1 < BS:
-                regroup_img(k // 2 + 1)
-                if k // 2 + 1 + RAW_BUFS - 1 < BS:
-                    load_img(k // 2 + RAW_BUFS)
-            if live(k - 3):
-                inv_colsum(k - 3)
-                spread_inv_colsum(k - 3)
-            if k % 2 == 1 and (k + 1) // 2 < BS:
-                quant_img((k + 1) // 2)
-            if live(k - 3):
-                row_of_col_attn(k - 3)
-            if live(k - 2):
-                exponent(k - 2)
-            if live(k - 1):
-                spread_inv_norm(k - 1)
-                normalise(k - 1)
-                quant_n(k - 1)
+        for k in range(-2, UNITS + 5):
             if live(k):
                 flip(k, 0)
-                flip(k, 1)
-                square_sum(k, 0)
-                flip(k, 2)
-                square_sum(k, 1)
-                flip(k, 3)
-                square_sum(k, 2)
-                square_sum(k, 3)
-                inv_norm(k)
             if live(k + 1):
-                for t in range(3):
-                    project(k + 1, t)
+                add_bias(k + 1, 0)
+                add_bias(k + 1, 1)
+            if k % 2 == 0 and 1 <= (k + 2) // 2 < BS:
+                quant_img((k + 2) // 2)
+            if live(k + 1):
+                add_bias(k + 1, 2)
+            if live(k - 2):
+                normalise(k - 2)
+            if live(k):
+                flip(k, 1)
+            if live(k + 1):
+                add_bias(k + 1, 3)
+            if live(k):
+                flip(k, 2)
+            if live(k - 4):
+                inv_colsum(k - 4)
+                spread_inv_colsum(k - 4)
+            if live(k - 2):
+                quant_n(k - 2)
+            if live(k):
+                square_sum(k, 0)
+                flip(k, 3)
+                square_sum(k, 1)
+            if live(k - 1):
+                spread_inv_norm(k - 1)
+            if live(k - 3):
+                inv_rowsum(k - 3)
+            if live(k):
+                square_sum(k, 2)
+            if live(k - 4):
+                row_of_col_attn(k - 4)
+            if k % 2 == 0 and 2 <= (k + 4) // 2 < BS:
+                regroup_img((k + 4) // 2)
+                if (k + 4) // 2 + RAW_BUFS < BS:
+                    load_img((k + 4) // 2 + RAW_BUFS)
+            if live(k - 2):
+                cosines(k - 2)
+            if live(k):
+                square_sum(k, 3)
+            if live(k + 2):
+                project(k + 2, 0)
+                project(k + 2, 1)
+            if live(k - 3):
+                column_sums(k - 3)
+            if live(k + 2):
+                project(k + 2, 2)
+                project(k + 2, 3)
+            if live(k - 2):
+                exponent(k - 2)
+            if live(k):
+                inv_norm(k)
 
         resv = res[:].rearrange("p (c f) -> p c f", f=2)
         tot = psfin.tile([P, 512], F32, tag="fin")
@@ -343,7 +355,7 @@ def tile_oaclipv3_t_kernel(tc, img1, img2, W, b, out):
             in1=rden[:].unsqueeze(2).to_broadcast([P, 64, 2]),
             op=ALU.mult,
         )
-        rt = pstr.tile([P, PACK * P], F32, tag="tr")
+        rt = ring.tile([P, PACK * P], F32, tag="feed")
         nc.tensor.transpose(out=rt[:, 0:P], in_=resn[:], identity=ident[:])
         o_sb = const.tile([P, P], F32)
         nc.vector.tensor_copy(out=o_sb[:], in_=rt[:, 0:P])

@@ -76,10 +76,20 @@ def tile_oaclipv3_t_kernel(tc, img1, img2, W, b, out):
         def regroup_img(i):
             xg = xgp.tile([P, 2, L, PACK], BF16, align_bytes=64)
             for s in range(2):
-                nc.vector.tensor_copy(
-                    out=xg[:, s].rearrange("p (c r) j -> p c j r", r=4),
-                    in_=raws[i][:, s].rearrange("p j (c r) -> p c j r", r=4),
-                )
+                if i < 2:
+                    nc.vector.tensor_copy(
+                        out=xg[:, s].rearrange("p (c r) j -> p c j r", r=4),
+                        in_=raws[i][:, s].rearrange("p j (c r) -> p c j r", r=4),
+                    )
+                else:
+                    nc.gpsimd.tensor_scalar(
+                        out=xg[:, s],
+                        in0=raws[i][:, s].rearrange("p j l -> p l j"),
+                        scalar1=1.0,
+                        scalar2=0.0,
+                        op0=ALU.mult,
+                        op1=ALU.add,
+                    )
             xgs[i] = xg
 
         def quant_img(i):
@@ -113,13 +123,15 @@ def tile_oaclipv3_t_kernel(tc, img1, img2, W, b, out):
             if t == 0:
                 qb = qbp.tile([P, PACK, NPOS], F32)
                 qbs[u] = qb
-            nc.scalar.activation(
-                out=qbs[u][:, t, :],
-                in_=qs[(u, t)][:],
-                func=ACT.Identity,
-                bias=b32[:, h * PACK + t : h * PACK + t + 1],
-                scale=1.0,
-            )
+            bcol = b32[:, h * PACK + t : h * PACK + t + 1]
+            if t == 3:
+                nc.vector.tensor_scalar(
+                    out=qbs[u][:, t, :], in0=qs[(u, t)][:], scalar1=bcol, scalar2=None, op0=ALU.add
+                )
+            else:
+                nc.scalar.activation(
+                    out=qbs[u][:, t, :], in_=qs[(u, t)][:], func=ACT.Identity, bias=bcol, scale=1.0
+                )
 
         def flip(u, c):
             tr = ring.tile([P, PACK * P], F32, tag="feed")
@@ -287,49 +299,52 @@ def tile_oaclipv3_t_kernel(tc, img1, img2, W, b, out):
         for k in range(-2, UNITS + 5):
             if live(k):
                 flip(k, 0)
-            if live(k + 1):
-                add_bias(k + 1, 0)
-                add_bias(k + 1, 1)
-            if k % 2 == 0 and 1 <= (k + 2) // 2 < BS:
-                quant_img((k + 2) // 2)
-            if live(k + 1):
-                add_bias(k + 1, 2)
             if live(k - 2):
                 normalise(k - 2)
+            if live(k + 1):
+                add_bias(k + 1, 0)
             if live(k):
                 flip(k, 1)
             if live(k + 1):
-                add_bias(k + 1, 3)
-            if live(k):
-                flip(k, 2)
+                add_bias(k + 1, 1)
+            if k % 2 == 0 and 1 <= (k + 2) // 2 < BS:
+                quant_img((k + 2) // 2)
             if live(k - 4):
                 inv_colsum(k - 4)
-                spread_inv_colsum(k - 4)
+            if live(k + 1):
+                add_bias(k + 1, 2)
             if live(k - 2):
                 quant_n(k - 2)
             if live(k):
+                flip(k, 2)
+            if live(k - 4):
+                spread_inv_colsum(k - 4)
+            if live(k):
                 square_sum(k, 0)
                 flip(k, 3)
-                square_sum(k, 1)
-            if live(k - 1):
-                spread_inv_norm(k - 1)
             if live(k - 3):
                 inv_rowsum(k - 3)
-            if live(k):
-                square_sum(k, 2)
-            if live(k - 4):
-                row_of_col_attn(k - 4)
-            if k % 2 == 0 and 2 <= (k + 4) // 2 < BS:
-                regroup_img((k + 4) // 2)
-                if (k + 4) // 2 + RAW_BUFS < BS:
-                    load_img((k + 4) // 2 + RAW_BUFS)
+            if live(k - 1):
+                spread_inv_norm(k - 1)
             if live(k - 2):
                 cosines(k - 2)
-            if live(k):
-                square_sum(k, 3)
+            if k % 2 == 1 and 2 <= (k + 5) // 2 < BS:
+                regroup_img((k + 5) // 2)
+                if (k + 5) // 2 + RAW_BUFS < BS:
+                    load_img((k + 5) // 2 + RAW_BUFS)
+            if live(k + 1):
+                add_bias(k + 1, 3)
             if live(k + 2):
                 project(k + 2, 0)
+            if live(k):
+                square_sum(k, 1)
+                square_sum(k, 2)
+            if live(k + 2):
                 project(k + 2, 1)
+            if live(k - 4):
+                row_of_col_attn(k - 4)
+            if live(k):
+                square_sum(k, 3)
             if live(k - 3):
                 column_sums(k - 3)
             if live(k + 2):

@@ -174,9 +174,12 @@ def tile_oaclipv3_t_kernel(tc, img1, img2, W, b, out):
         def normalise(u):
             ng = ngp.tile([P, NPOS, PACK], BF16, align_bytes=64)
             nc.vector.tensor_tensor(
-                out=ng[:],
-                in0=qbs[u][:].rearrange("p t c -> p c t"),
-                in1=rbcs[u][:].unsqueeze(2).to_broadcast([P, NPOS, PACK]),
+                out=ng[:].rearrange("p (c r) t -> p c t r", r=4),
+                in0=qbs[u][:].rearrange("p t (c r) -> p c t r", r=4),
+                in1=rbcs[u][:]
+                .rearrange("p (c r) -> p c r", r=4)
+                .unsqueeze(2)
+                .to_broadcast([P, NPOS // 4, PACK, 4]),
                 op=ALU.mult,
             )
             ngs[u] = ng

@@ -19,6 +19,7 @@ UNITS = BS * H
 LAMBDA = 10.0
 FLOPS = 2 * (2 * BS * L) * D * (H * E) + 2 * H * BS * L * L * E
 W2_SLOTS = 4
+MV_COLS = 64
 RAW_BUFS = 4
 
 
@@ -45,7 +46,7 @@ def tile_oaclipv3_t_kernel(tc, img1, img2, W, b, out):
         ident = const.tile([P, P], F32)
         ones = const.tile([P, P], F32)
         mhalf = const.tile([P, 4], F32)
-        w2 = const.tile([P, W2_SLOTS, 2, 2], F32)
+        w2 = const.tile([P, W2_SLOTS, 2, MV_COLS], F32)
         res = const.tile([P, 128], F32)
         b32 = const.tile([P, H * PACK], F32)
         w_grp = const.tile([P, H, PACK, P, PACK], BF16, align_bytes=64)
@@ -232,7 +233,7 @@ def tile_oaclipv3_t_kernel(tc, img1, img2, W, b, out):
             for mb in range(2):
                 for lb in range(2):
                     nc.tensor.matmul(
-                        out=fin[:, L + 2 * mb : L + 2 * mb + 2],
+                        out=fin[:, L + MV_COLS * mb : L + MV_COLS * (mb + 1)],
                         lhsT=exs[u][:, lb, mb * P : (mb + 1) * P],
                         rhs=w2[:, u % W2_SLOTS, lb, :],
                         start=(lb == 0),
@@ -242,7 +243,7 @@ def tile_oaclipv3_t_kernel(tc, img1, img2, W, b, out):
 
         def inv_colsum(u):
             i, h = divmod(u, H)
-            cs = fins[u][:, L : L + 4].rearrange("p (m k) -> p m k", k=2)
+            cs = fins[u][:, L : L + 2 * MV_COLS].rearrange("p (m k) -> p m k", k=MV_COLS)
             rc = smallp.tile([P, 2], F32)
             nc.vector.reciprocal(out=rc[:], in_=cs[:, :, 0])
             col12 = ((2 + h) * BS + i) * 2
@@ -300,63 +301,63 @@ def tile_oaclipv3_t_kernel(tc, img1, img2, W, b, out):
         quant_w(1)
 
         for k in range(-2, UNITS + 5):
-            if live(k):
-                flip(k, 0)
+            if live(k + 1):
+                project(k + 1, 0)
+                project(k + 1, 1)
+                add_bias(k + 1, 0)
             if live(k - 2):
                 normalise(k - 2)
             if live(k + 1):
-                add_bias(k + 1, 0)
+                add_bias(k + 1, 1)
+            if live(k - 3):
+                inv_rowsum(k - 3)
+            if live(k):
+                flip(k, 0)
+            if live(k - 4):
+                inv_colsum(k - 4)
             if live(k):
                 flip(k, 1)
             if live(k + 1):
-                add_bias(k + 1, 1)
-            if k % 2 == 0 and 1 <= (k + 2) // 2 < BS:
-                quant_img((k + 2) // 2)
-            if live(k - 4):
-                inv_colsum(k - 4)
-            if live(k + 1):
-                add_bias(k + 1, 2)
+                project(k + 1, 2)
+                project(k + 1, 3)
+            if k % 2 == 0 and 2 <= (k + 6) // 2 < BS:
+                regroup_img((k + 6) // 2)
+                if (k + 6) // 2 + RAW_BUFS < BS:
+                    load_img((k + 6) // 2 + RAW_BUFS)
+            if live(k):
+                square_sum(k, 0)
             if live(k - 2):
                 quant_n(k - 2)
-            if live(k):
-                flip(k, 2)
             if live(k - 4):
                 spread_inv_colsum(k - 4)
             if live(k):
-                square_sum(k, 0)
-                flip(k, 3)
-            if live(k - 3):
-                inv_rowsum(k - 3)
-            if live(k - 1):
-                spread_inv_norm(k - 1)
-            if live(k - 2):
-                cosines(k - 2)
-            if k % 2 == 1 and 2 <= (k + 5) // 2 < BS:
-                regroup_img((k + 5) // 2)
-                if (k + 5) // 2 + RAW_BUFS < BS:
-                    load_img((k + 5) // 2 + RAW_BUFS)
+                flip(k, 2)
             if live(k + 1):
                 add_bias(k + 1, 3)
-            if live(k + 2):
-                project(k + 2, 0)
             if live(k):
                 square_sum(k, 1)
-                square_sum(k, 2)
-            if live(k + 2):
-                project(k + 2, 1)
+            if live(k - 1):
+                spread_inv_norm(k - 1)
+            if live(k):
+                flip(k, 3)
             if live(k - 4):
                 row_of_col_attn(k - 4)
+            if live(k + 1):
+                add_bias(k + 1, 2)
+            if live(k):
+                square_sum(k, 2)
+            if live(k - 2):
+                cosines(k - 2)
+            if k % 2 == 1 and 1 <= (k + 3) // 2 < BS:
+                quant_img((k + 3) // 2)
             if live(k):
                 square_sum(k, 3)
-            if live(k - 3):
-                column_sums(k - 3)
-            if live(k + 2):
-                project(k + 2, 2)
-                project(k + 2, 3)
             if live(k - 2):
                 exponent(k - 2)
             if live(k):
                 inv_norm(k)
+            if live(k - 3):
+                column_sums(k - 3)
 
         resv = res[:].rearrange("p (c f) -> p c f", f=2)
         tot = psfin.tile([P, 512], F32, tag="fin")

@@ -34,7 +34,7 @@ def tile_oaclipv3_t_kernel(tc, img1, img2, W, b, out):
         junkp = ctx.enter_context(tc.tile_pool(name="junkp", bufs=2))
         ngp = ctx.enter_context(tc.tile_pool(name="ngp", bufs=3))
         ncp = ctx.enter_context(tc.tile_pool(name="ncp", bufs=3))
-        ep = ctx.enter_context(tc.tile_pool(name="ep", bufs=4))
+        ep = ctx.enter_context(tc.tile_pool(name="ep", bufs=5))
         smallp = ctx.enter_context(tc.tile_pool(name="smallp", bufs=4))
         ring = ctx.enter_context(tc.psum_pool(name="ring", bufs=6))
         psr = ctx.enter_context(tc.psum_pool(name="psr", bufs=1))
@@ -55,7 +55,8 @@ def tile_oaclipv3_t_kernel(tc, img1, img2, W, b, out):
 
         raws, xgs, xcs, xss = {}, {}, {}, {}
         qs, qbs, trs, nrms, rns, rbcs, ngs, ncods, nscls = {}, {}, {}, {}, {}, {}, {}, {}, {}
-        rels, exs, rss, fins, rcs = {}, {}, {}, {}, {}
+        rels, exs, rss, rcs = {}, {}, {}, {}
+        fin = psfin.tile([P, 512], F32)
 
         def load_w(h):
             nc.sync.dma_start(out=w_raw[:, h], in_=W[h].rearrange("(p j) e -> p j e", j=PACK))
@@ -229,21 +230,21 @@ def tile_oaclipv3_t_kernel(tc, img1, img2, W, b, out):
             nc.vector.reciprocal(out=w2[:, u % W2_SLOTS, :, 1], in_=rss[u][:])
 
         def column_sums(u):
-            fin = psfin.tile([P, 512], F32)
+            base = L + (u % 2) * 2 * MV_COLS
             for mb in range(2):
                 for lb in range(2):
                     nc.tensor.matmul(
-                        out=fin[:, L + MV_COLS * mb : L + MV_COLS * (mb + 1)],
+                        out=fin[:, base + MV_COLS * mb : base + MV_COLS * (mb + 1)],
                         lhsT=exs[u][:, lb, mb * P : (mb + 1) * P],
                         rhs=w2[:, u % W2_SLOTS, lb, :],
                         start=(lb == 0),
                         stop=(lb == 1),
                     )
-            fins[u] = fin
 
         def inv_colsum(u):
             i, h = divmod(u, H)
-            cs = fins[u][:, L : L + 2 * MV_COLS].rearrange("p (m k) -> p m k", k=MV_COLS)
+            base = L + (u % 2) * 2 * MV_COLS
+            cs = fin[:, base : base + 2 * MV_COLS].rearrange("p (m k) -> p m k", k=MV_COLS)
             rc = smallp.tile([P, 2], F32)
             nc.vector.reciprocal(out=rc[:], in_=cs[:, :, 0])
             col12 = ((2 + h) * BS + i) * 2
@@ -253,7 +254,7 @@ def tile_oaclipv3_t_kernel(tc, img1, img2, W, b, out):
         def spread_inv_colsum(u):
             for mb in range(2):
                 nc.tensor.transpose(
-                    out=fins[u][:, mb * P : (mb + 1) * P],
+                    out=fin[:, mb * P : (mb + 1) * P],
                     in_=rcs[u][:, mb : mb + 1].to_broadcast([P, P]),
                     identity=ident[:],
                 )
@@ -267,7 +268,7 @@ def tile_oaclipv3_t_kernel(tc, img1, img2, W, b, out):
                     out=pj[:],
                     in0=exs[u][:, lb, :],
                     scalar=1.0,
-                    in1=fins[u][:, 0:L],
+                    in1=fin[:, 0:L],
                     op0=ALU.mult,
                     op1=ALU.mult,
                     accum_out=res[:, col21 + lb : col21 + lb + 1],
@@ -288,9 +289,13 @@ def tile_oaclipv3_t_kernel(tc, img1, img2, W, b, out):
         nc.vector.memset(w2[:], 1.0)
         nc.vector.memset(ones[:], 1.0)
         nc.vector.tensor_copy(
-            out=w_grp[:, 0], in_=w_raw[:, 0].rearrange("p j (m t) -> p t m j", t=PACK)
+            out=w_grp[:, 0].rearrange("p t m j -> p m j t"),
+            in_=w_raw[:, 0].rearrange("p j (m t) -> p m j t", t=PACK),
         )
-        nc.scalar.copy(out=w_grp[:, 1], in_=w_raw[:, 1].rearrange("p j (m t) -> p t m j", t=PACK))
+        nc.scalar.copy(
+            out=w_grp[:, 1].rearrange("p t m j -> p m j t"),
+            in_=w_raw[:, 1].rearrange("p j (m t) -> p m j t", t=PACK),
+        )
         regroup_img(0)
         load_img(RAW_BUFS)
         quant_w(0)
@@ -300,7 +305,9 @@ def tile_oaclipv3_t_kernel(tc, img1, img2, W, b, out):
         load_img(RAW_BUFS + 1)
         quant_w(1)
 
-        for k in range(-2, UNITS + 5):
+        for k in range(-2, UNITS + 6):
+            if live(k - 5):
+                row_of_col_attn(k - 5)
             if live(k + 1):
                 project(k + 1, 0)
                 project(k + 1, 1)
@@ -340,8 +347,6 @@ def tile_oaclipv3_t_kernel(tc, img1, img2, W, b, out):
                 spread_inv_norm(k - 1)
             if live(k):
                 flip(k, 3)
-            if live(k - 4):
-                row_of_col_attn(k - 4)
             if live(k + 1):
                 add_bias(k + 1, 2)
             if live(k):
@@ -360,22 +365,24 @@ def tile_oaclipv3_t_kernel(tc, img1, img2, W, b, out):
                 column_sums(k - 3)
 
         resv = res[:].rearrange("p (c f) -> p c f", f=2)
-        tot = psfin.tile([P, 512], F32, tag="fin")
-        nc.tensor.matmul(out=tot[:, 0:64], lhsT=ones[:], rhs=resv[:, :, 0], start=True, stop=False)
-        nc.tensor.matmul(out=tot[:, 0:64], lhsT=ones[:], rhs=resv[:, :, 1], start=False, stop=True)
-        den = const.tile([P, 64], F32)
-        nc.vector.tensor_scalar(out=den[:], in0=tot[:, 0:64], scalar1=1e-8, scalar2=None, op0=ALU.add)
-        rden = const.tile([P, 64], F32)
-        nc.vector.reciprocal(out=rden[:], in_=den[:])
-        resn = const.tile([P, 128], F32)
+        pair = const.tile([P, 128], F32)
         nc.vector.tensor_tensor(
-            out=resn[:].rearrange("p (c f) -> p c f", f=2),
-            in0=resv,
-            in1=rden[:].unsqueeze(2).to_broadcast([P, 64, 2]),
-            op=ALU.mult,
+            out=pair[:].rearrange("p (c f) -> p c f", f=2),
+            in0=resv[:, :, 0:1].to_broadcast([P, 64, 2]),
+            in1=resv[:, :, 1:2].to_broadcast([P, 64, 2]),
+            op=ALU.add,
         )
         rt = ring.tile([P, PACK * P], F32, tag="feed")
-        nc.tensor.transpose(out=rt[:, 0:P], in_=resn[:], identity=ident[:])
+        nc.tensor.transpose(out=rt[:, 0:P], in_=res[:], identity=ident[:])
+        nc.tensor.matmul(out=rt[:, P : P + 2], lhsT=pair[:], rhs=ones[:, 0:2], start=True, stop=True)
+        den = const.tile([P, 1], F32)
+        nc.vector.tensor_scalar(
+            out=den[:], in0=rt[:, P : P + 1], scalar1=1e-8, scalar2=None, op0=ALU.add
+        )
+        rden = const.tile([P, 1], F32)
+        nc.vector.reciprocal(out=rden[:], in_=den[:])
         o_sb = const.tile([P, P], F32)
-        nc.vector.tensor_copy(out=o_sb[:], in_=rt[:, 0:P])
+        nc.vector.tensor_scalar(
+            out=o_sb[:], in0=rt[:, 0:P], scalar1=rden[:, 0:1], scalar2=None, op0=ALU.mult
+        )
         nc.sync.dma_start(out=out.rearrange("w h i (f p) -> (w h i f) p", p=P), in_=o_sb[:])

@@ -34,7 +34,7 @@ def tile_oaclipv3_t_kernel(tc, img1, img2, W, b, out):
         junkp = ctx.enter_context(tc.tile_pool(name="junkp", bufs=2))
         ngp = ctx.enter_context(tc.tile_pool(name="ngp", bufs=3))
         ncp = ctx.enter_context(tc.tile_pool(name="ncp", bufs=3))
-        ep = ctx.enter_context(tc.tile_pool(name="ep", bufs=5))
+        ep = ctx.enter_context(tc.tile_pool(name="ep", bufs=4))
         smallp = ctx.enter_context(tc.tile_pool(name="smallp", bufs=4))
         ring = ctx.enter_context(tc.psum_pool(name="ring", bufs=6))
         psr = ctx.enter_context(tc.psum_pool(name="psr", bufs=1))
@@ -55,8 +55,7 @@ def tile_oaclipv3_t_kernel(tc, img1, img2, W, b, out):
 
         raws, xgs, xcs, xss = {}, {}, {}, {}
         qs, qbs, trs, nrms, rns, rbcs, ngs, ncods, nscls = {}, {}, {}, {}, {}, {}, {}, {}, {}
-        rels, exs, rss, rcs = {}, {}, {}, {}
-        fin = psfin.tile([P, 512], F32)
+        rels, exs, rss, fins, rcs = {}, {}, {}, {}, {}
 
         def load_w(h):
             nc.sync.dma_start(out=w_raw[:, h], in_=W[h].rearrange("(p j) e -> p j e", j=PACK))
@@ -230,21 +229,24 @@ def tile_oaclipv3_t_kernel(tc, img1, img2, W, b, out):
             nc.vector.reciprocal(out=w2[:, u % W2_SLOTS, :, 1], in_=rss[u][:])
 
         def column_sums(u):
-            base = L + (u % 2) * 2 * MV_COLS
+            if u < UNITS - 2:
+                fin = psfin.tile([P, 512], F32)
+            else:
+                fin = ring.tile([P, 512], F32, tag="feed")
             for mb in range(2):
                 for lb in range(2):
                     nc.tensor.matmul(
-                        out=fin[:, base + MV_COLS * mb : base + MV_COLS * (mb + 1)],
+                        out=fin[:, L + MV_COLS * mb : L + MV_COLS * (mb + 1)],
                         lhsT=exs[u][:, lb, mb * P : (mb + 1) * P],
                         rhs=w2[:, u % W2_SLOTS, lb, :],
                         start=(lb == 0),
                         stop=(lb == 1),
                     )
+            fins[u] = fin
 
         def inv_colsum(u):
             i, h = divmod(u, H)
-            base = L + (u % 2) * 2 * MV_COLS
-            cs = fin[:, base : base + 2 * MV_COLS].rearrange("p (m k) -> p m k", k=MV_COLS)
+            cs = fins[u][:, L : L + 2 * MV_COLS].rearrange("p (m k) -> p m k", k=MV_COLS)
             rc = smallp.tile([P, 2], F32)
             nc.vector.reciprocal(out=rc[:], in_=cs[:, :, 0])
             col12 = ((2 + h) * BS + i) * 2
@@ -254,7 +256,7 @@ def tile_oaclipv3_t_kernel(tc, img1, img2, W, b, out):
         def spread_inv_colsum(u):
             for mb in range(2):
                 nc.tensor.transpose(
-                    out=fin[:, mb * P : (mb + 1) * P],
+                    out=fins[u][:, mb * P : (mb + 1) * P],
                     in_=rcs[u][:, mb : mb + 1].to_broadcast([P, P]),
                     identity=ident[:],
                 )
@@ -268,7 +270,7 @@ def tile_oaclipv3_t_kernel(tc, img1, img2, W, b, out):
                     out=pj[:],
                     in0=exs[u][:, lb, :],
                     scalar=1.0,
-                    in1=fin[:, 0:L],
+                    in1=fins[u][:, 0:L],
                     op0=ALU.mult,
                     op1=ALU.mult,
                     accum_out=res[:, col21 + lb : col21 + lb + 1],
@@ -305,9 +307,7 @@ def tile_oaclipv3_t_kernel(tc, img1, img2, W, b, out):
         load_img(RAW_BUFS + 1)
         quant_w(1)
 
-        for k in range(-2, UNITS + 6):
-            if live(k - 5):
-                row_of_col_attn(k - 5)
+        for k in range(-2, UNITS + 5):
             if live(k + 1):
                 project(k + 1, 0)
                 project(k + 1, 1)
@@ -347,6 +347,8 @@ def tile_oaclipv3_t_kernel(tc, img1, img2, W, b, out):
                 spread_inv_norm(k - 1)
             if live(k):
                 flip(k, 3)
+            if live(k - 4):
+                row_of_col_attn(k - 4)
             if live(k + 1):
                 add_bias(k + 1, 2)
             if live(k):

@@ -21,6 +21,7 @@ FLOPS = 2 * (2 * BS * L) * D * (H * E) + 2 * H * BS * L * L * E
 W2_SLOTS = 4
 MV_COLS = 64
 RAW_BUFS = 4
+FILL = 3
 
 
 def tile_oaclipv3_t_kernel(tc, img1, img2, W, b, out):
@@ -28,9 +29,9 @@ def tile_oaclipv3_t_kernel(tc, img1, img2, W, b, out):
     with ExitStack() as ctx:
         const = ctx.enter_context(tc.tile_pool(name="const", bufs=1))
         rawp = ctx.enter_context(tc.tile_pool(name="rawp", bufs=RAW_BUFS))
-        xgp = ctx.enter_context(tc.tile_pool(name="xgp", bufs=2))
+        xgp = ctx.enter_context(tc.tile_pool(name="xgp", bufs=3))
         xcp = ctx.enter_context(tc.tile_pool(name="xcp", bufs=3))
-        qbp = ctx.enter_context(tc.tile_pool(name="qbp", bufs=5))
+        qbp = ctx.enter_context(tc.tile_pool(name="qbp", bufs=6))
         junkp = ctx.enter_context(tc.tile_pool(name="junkp", bufs=2))
         ngp = ctx.enter_context(tc.tile_pool(name="ngp", bufs=3))
         ncp = ctx.enter_context(tc.tile_pool(name="ncp", bufs=3))
@@ -48,6 +49,7 @@ def tile_oaclipv3_t_kernel(tc, img1, img2, W, b, out):
         mhalf = const.tile([P, 4], F32)
         w2 = const.tile([P, W2_SLOTS, 2, MV_COLS], F32)
         res = const.tile([P, 128], F32)
+        rcs = const.tile([P, H, BS, 2, 2], F32)
         b32 = const.tile([P, H * PACK], F32)
         w_grp = const.tile([P, H, PACK, P, PACK], BF16, align_bytes=64)
         w_cod = const.tile([P, H * PACK * P], U32, align_bytes=64)
@@ -55,7 +57,7 @@ def tile_oaclipv3_t_kernel(tc, img1, img2, W, b, out):
 
         raws, xgs, xcs, xss = {}, {}, {}, {}
         qs, qbs, trs, nrms, rns, rbcs, ngs, ncods, nscls = {}, {}, {}, {}, {}, {}, {}, {}, {}
-        rels, exs, rss, fins, rcs = {}, {}, {}, {}, {}
+        rels, exs, rss, fins = {}, {}, {}, {}
 
         def load_w(h):
             nc.sync.dma_start(out=w_raw[:, h], in_=W[h].rearrange("(p j) e -> p j e", j=PACK))
@@ -66,12 +68,17 @@ def tile_oaclipv3_t_kernel(tc, img1, img2, W, b, out):
             nc.sync.dma_start(out=raw[:, 1], in_=img2[i].rearrange("(p j) l -> p j l", j=PACK))
             raws[i] = raw
 
-        def quant_w(h):
-            cols = slice(h * PACK * P, (h + 1) * PACK * P)
+        def regroup_w(h, t0, t1):
+            dst = w_grp[:, h, t0:t1].rearrange("p t m j -> p m j t")
+            src = w_raw[:, h].rearrange("p j (m t) -> p m j t", t=PACK)[:, :, :, t0:t1]
+            nc.vector.tensor_copy(out=dst, in_=src)
+
+        def quant_w(h, t0, t1):
+            cols = slice((h * PACK + t0) * P, (h * PACK + t1) * P)
             nc.vector.quantize_mx(
                 out=w_cod[:, cols].bitcast(FP8X4),
                 scales=w_scl[:, cols],
-                in_=w_grp[:, h].rearrange("p t m j -> p (t m j)"),
+                in_=w_grp[:, h, t0:t1].rearrange("p t m j -> p (t m j)"),
             )
 
         def regroup_img(i):
@@ -125,7 +132,7 @@ def tile_oaclipv3_t_kernel(tc, img1, img2, W, b, out):
                 qb = qbp.tile([P, PACK, NPOS], F32)
                 qbs[u] = qb
             bcol = b32[:, h * PACK + t : h * PACK + t + 1]
-            if t == 3:
+            if t == 3 or (t == 1 and u < FILL):
                 nc.vector.tensor_scalar(
                     out=qbs[u][:, t, :], in0=qs[(u, t)][:], scalar1=bcol, scalar2=None, op0=ALU.add
                 )
@@ -247,17 +254,14 @@ def tile_oaclipv3_t_kernel(tc, img1, img2, W, b, out):
         def inv_colsum(u):
             i, h = divmod(u, H)
             cs = fins[u][:, L : L + 2 * MV_COLS].rearrange("p (m k) -> p m k", k=MV_COLS)
-            rc = smallp.tile([P, 2], F32)
-            nc.vector.reciprocal(out=rc[:], in_=cs[:, :, 0])
-            col12 = ((2 + h) * BS + i) * 2
-            nc.vector.tensor_copy(out=res[:, col12 : col12 + 2], in_=cs[:, :, 1])
-            rcs[u] = rc
+            nc.vector.reciprocal(out=rcs[:, h, i, :, :], in_=cs[:, :, 0:2])
 
         def spread_inv_colsum(u):
+            i, h = divmod(u, H)
             for mb in range(2):
                 nc.tensor.transpose(
                     out=fins[u][:, mb * P : (mb + 1) * P],
-                    in_=rcs[u][:, mb : mb + 1].to_broadcast([P, P]),
+                    in_=rcs[:, h, i, mb, 0:1].to_broadcast([P, P]),
                     identity=ident[:],
                 )
 
@@ -290,38 +294,43 @@ def tile_oaclipv3_t_kernel(tc, img1, img2, W, b, out):
         nc.vector.memset(mhalf[:], -0.5)
         nc.vector.memset(w2[:], 1.0)
         nc.vector.memset(ones[:], 1.0)
-        nc.vector.tensor_copy(
-            out=w_grp[:, 0].rearrange("p t m j -> p m j t"),
-            in_=w_raw[:, 0].rearrange("p j (m t) -> p m j t", t=PACK),
+        nc.gpsimd.tensor_scalar(
+            out=w_grp[:, 1, 2:PACK],
+            in0=w_raw[:, 1].rearrange("p j (m t) -> p t m j", t=PACK)[:, 2:PACK],
+            scalar1=1.0,
+            scalar2=0.0,
+            op0=ALU.mult,
+            op1=ALU.add,
         )
+        nc.scalar.copy(out=b32[:], in_=b_raw[:].rearrange("p h t -> p (h t)"))
         nc.scalar.copy(
-            out=w_grp[:, 1].rearrange("p t m j -> p m j t"),
-            in_=w_raw[:, 1].rearrange("p j (m t) -> p m j t", t=PACK),
+            out=w_grp[:, 1, 0:2].rearrange("p t m j -> p m j t"),
+            in_=w_raw[:, 1].rearrange("p j (m t) -> p m j t", t=PACK)[:, :, :, 0:2],
         )
+        regroup_w(0, 0, 2)
         regroup_img(0)
         load_img(RAW_BUFS)
-        quant_w(0)
+        quant_w(0, 0, 2)
         quant_img(0)
-        nc.vector.tensor_copy(out=b32[:], in_=b_raw[:].rearrange("p h t -> p (h t)"))
-        regroup_img(1)
-        load_img(RAW_BUFS + 1)
-        quant_w(1)
+        regroup_w(0, 2, PACK)
+        quant_w(0, 2, PACK)
+        quant_w(1, 0, PACK)
 
-        for k in range(-2, UNITS + 5):
+        for k in range(-2, UNITS + 6):
             if live(k + 1):
                 project(k + 1, 0)
                 project(k + 1, 1)
                 add_bias(k + 1, 0)
-            if live(k - 2):
-                normalise(k - 2)
+            if live(k - 3):
+                normalise(k - 3)
             if live(k + 1):
                 add_bias(k + 1, 1)
-            if live(k - 3):
-                inv_rowsum(k - 3)
+            if live(k - 4):
+                inv_rowsum(k - 4)
             if live(k):
                 flip(k, 0)
-            if live(k - 4):
-                inv_colsum(k - 4)
+            if live(k - 5):
+                inv_colsum(k - 5)
             if live(k):
                 flip(k, 1)
             if live(k + 1):
@@ -333,39 +342,46 @@ def tile_oaclipv3_t_kernel(tc, img1, img2, W, b, out):
                     load_img((k + 6) // 2 + RAW_BUFS)
             if live(k):
                 square_sum(k, 0)
-            if live(k - 2):
-                quant_n(k - 2)
-            if live(k - 4):
-                spread_inv_colsum(k - 4)
+            if live(k - 3):
+                quant_n(k - 3)
+            if live(k - 5):
+                spread_inv_colsum(k - 5)
             if live(k):
                 flip(k, 2)
             if live(k + 1):
                 add_bias(k + 1, 3)
             if live(k):
                 square_sum(k, 1)
-            if live(k - 1):
-                spread_inv_norm(k - 1)
+            if live(k - 2):
+                spread_inv_norm(k - 2)
             if live(k):
                 flip(k, 3)
-            if live(k - 4):
-                row_of_col_attn(k - 4)
+            if live(k - 5):
+                row_of_col_attn(k - 5)
             if live(k + 1):
                 add_bias(k + 1, 2)
             if live(k):
                 square_sum(k, 2)
-            if live(k - 2):
-                cosines(k - 2)
+            if live(k - 3):
+                cosines(k - 3)
+            if k == -1:
+                regroup_img(1)
+                load_img(RAW_BUFS + 1)
             if k % 2 == 1 and 1 <= (k + 3) // 2 < BS:
                 quant_img((k + 3) // 2)
             if live(k):
                 square_sum(k, 3)
-            if live(k - 2):
-                exponent(k - 2)
+            if live(k - 3):
+                exponent(k - 3)
             if live(k):
                 inv_norm(k)
-            if live(k - 3):
-                column_sums(k - 3)
+            if live(k - 4):
+                column_sums(k - 4)
 
+        nc.vector.reciprocal(
+            out=res[:, 64:128].rearrange("p (c f) -> p c f", f=2),
+            in_=rcs[:].rearrange("p h i m k -> p (h i) m k")[:, :, :, 1],
+        )
         resv = res[:].rearrange("p (c f) -> p c f", f=2)
         pair = const.tile([P, 128], F32)
         nc.vector.tensor_tensor(

@@ -21,7 +21,7 @@ FLOPS = 2 * (2 * BS * L) * D * (H * E) + 2 * H * BS * L * L * E
 W2_SLOTS = 4
 MV_COLS = 64
 RAW_BUFS = 4
-FILL = 3
+FILL = 4
 
 
 def tile_oaclipv3_t_kernel(tc, img1, img2, W, b, out):
@@ -68,37 +68,38 @@ def tile_oaclipv3_t_kernel(tc, img1, img2, W, b, out):
             nc.sync.dma_start(out=raw[:, 1], in_=img2[i].rearrange("(p j) l -> p j l", j=PACK))
             raws[i] = raw
 
-        def regroup_w(h, t0, t1):
-            dst = w_grp[:, h, t0:t1].rearrange("p t m j -> p m j t")
-            src = w_raw[:, h].rearrange("p j (m t) -> p m j t", t=PACK)[:, :, :, t0:t1]
-            nc.vector.tensor_copy(out=dst, in_=src)
-
-        def quant_w(h, t0, t1):
-            cols = slice((h * PACK + t0) * P, (h * PACK + t1) * P)
+        def quant_w(h):
+            cols = slice(h * PACK * P, (h + 1) * PACK * P)
             nc.vector.quantize_mx(
                 out=w_cod[:, cols].bitcast(FP8X4),
                 scales=w_scl[:, cols],
-                in_=w_grp[:, h, t0:t1].rearrange("p t m j -> p (t m j)"),
+                in_=w_grp[:, h].rearrange("p t m j -> p (t m j)"),
             )
 
-        def regroup_img(i):
-            xg = xgp.tile([P, 2, L, PACK], BF16, align_bytes=64)
-            for s in range(2):
-                if i < 2:
-                    nc.vector.tensor_copy(
-                        out=xg[:, s].rearrange("p (c r) j -> p c j r", r=4),
-                        in_=raws[i][:, s].rearrange("p j (c r) -> p c j r", r=4),
-                    )
-                else:
-                    nc.gpsimd.tensor_scalar(
-                        out=xg[:, s],
-                        in0=raws[i][:, s].rearrange("p j l -> p l j"),
-                        scalar1=1.0,
-                        scalar2=0.0,
-                        op0=ALU.mult,
-                        op1=ALU.add,
-                    )
-            xgs[i] = xg
+        def gate_regroup(i, s):
+            if s == 0:
+                xg = xgp.tile([P, 2, L, PACK], BF16, align_bytes=64)
+                xgs[i] = xg
+            nc.vector.memset(xgs[i][:, s, 0:1, :], 0.0)
+
+        def regroup_img(i, s):
+            if i < 2:
+                if s == 0:
+                    xg = xgp.tile([P, 2, L, PACK], BF16, align_bytes=64)
+                    xgs[i] = xg
+                nc.vector.tensor_copy(
+                    out=xgs[i][:, s].rearrange("p (c r) j -> p c j r", r=4),
+                    in_=raws[i][:, s].rearrange("p j (c r) -> p c j r", r=4),
+                )
+            else:
+                nc.gpsimd.tensor_scalar(
+                    out=xgs[i][:, s],
+                    in0=raws[i][:, s].rearrange("p j l -> p l j"),
+                    scalar1=1.0,
+                    scalar2=0.0,
+                    op0=ALU.mult,
+                    op1=ALU.add,
+                )
 
         def quant_img(i):
             xc = xcp.tile([P, NPOS], U32, align_bytes=64)
@@ -294,27 +295,24 @@ def tile_oaclipv3_t_kernel(tc, img1, img2, W, b, out):
         nc.vector.memset(mhalf[:], -0.5)
         nc.vector.memset(w2[:], 1.0)
         nc.vector.memset(ones[:], 1.0)
-        nc.gpsimd.tensor_scalar(
-            out=w_grp[:, 1, 2:PACK],
-            in0=w_raw[:, 1].rearrange("p j (m t) -> p t m j", t=PACK)[:, 2:PACK],
-            scalar1=1.0,
-            scalar2=0.0,
-            op0=ALU.mult,
-            op1=ALU.add,
+        nc.vector.tensor_copy(
+            out=w_grp[:, 0].rearrange("p t m j -> p m j t"),
+            in_=w_raw[:, 0].rearrange("p j (m t) -> p m j t", t=PACK),
         )
-        nc.scalar.copy(out=b32[:], in_=b_raw[:].rearrange("p h t -> p (h t)"))
         nc.scalar.copy(
-            out=w_grp[:, 1, 0:2].rearrange("p t m j -> p m j t"),
-            in_=w_raw[:, 1].rearrange("p j (m t) -> p m j t", t=PACK)[:, :, :, 0:2],
+            out=w_grp[:, 1].rearrange("p t m j -> p m j t"),
+            in_=w_raw[:, 1].rearrange("p j (m t) -> p m j t", t=PACK),
         )
-        regroup_w(0, 0, 2)
-        regroup_img(0)
+        regroup_img(0, 0)
+        regroup_img(0, 1)
         load_img(RAW_BUFS)
-        quant_w(0, 0, 2)
+        quant_w(0)
         quant_img(0)
-        regroup_w(0, 2, PACK)
-        quant_w(0, 2, PACK)
-        quant_w(1, 0, PACK)
+        nc.vector.tensor_copy(out=b32[:], in_=b_raw[:].rearrange("p h t -> p (h t)"))
+        regroup_img(1, 0)
+        regroup_img(1, 1)
+        load_img(RAW_BUFS + 1)
+        quant_w(1)
 
         for k in range(-2, UNITS + 6):
             if live(k + 1):
@@ -336,14 +334,18 @@ def tile_oaclipv3_t_kernel(tc, img1, img2, W, b, out):
             if live(k + 1):
                 project(k + 1, 2)
                 project(k + 1, 3)
-            if k % 2 == 0 and 2 <= (k + 6) // 2 < BS:
-                regroup_img((k + 6) // 2)
-                if (k + 6) // 2 + RAW_BUFS < BS:
-                    load_img((k + 6) // 2 + RAW_BUFS)
             if live(k):
                 square_sum(k, 0)
             if live(k - 3):
                 quant_n(k - 3)
+            if k % 2 == 1 and 1 <= (k + 3) // 2 < BS:
+                quant_img((k + 3) // 2)
+            i = (k + 6) // 2 if k % 2 == 0 else (k + 5) // 2
+            if 2 <= i < BS:
+                gate_regroup(i, k % 2)
+                regroup_img(i, k % 2)
+                if k % 2 == 1 and i + RAW_BUFS < BS:
+                    load_img(i + RAW_BUFS)
             if live(k - 5):
                 spread_inv_colsum(k - 5)
             if live(k):
@@ -364,11 +366,6 @@ def tile_oaclipv3_t_kernel(tc, img1, img2, W, b, out):
                 square_sum(k, 2)
             if live(k - 3):
                 cosines(k - 3)
-            if k == -1:
-                regroup_img(1)
-                load_img(RAW_BUFS + 1)
-            if k % 2 == 1 and 1 <= (k + 3) // 2 < BS:
-                quant_img((k + 3) // 2)
             if live(k):
                 square_sum(k, 3)
             if live(k - 3):

@@ -21,7 +21,7 @@ FLOPS = 2 * (2 * BS * L) * D * (H * E) + 2 * H * BS * L * L * E
 W2_SLOTS = 4
 MV_COLS = 64
 RAW_BUFS = 4
-FILL = 4
+FILL = 5
 
 
 def tile_oaclipv3_t_kernel(tc, img1, img2, W, b, out):
@@ -49,7 +49,6 @@ def tile_oaclipv3_t_kernel(tc, img1, img2, W, b, out):
         mhalf = const.tile([P, 4], F32)
         w2 = const.tile([P, W2_SLOTS, 2, MV_COLS], F32)
         res = const.tile([P, 128], F32)
-        rcs = const.tile([P, H, BS, 2, 2], F32)
         b32 = const.tile([P, H * PACK], F32)
         w_grp = const.tile([P, H, PACK, P, PACK], BF16, align_bytes=64)
         w_cod = const.tile([P, H * PACK * P], U32, align_bytes=64)
@@ -57,7 +56,7 @@ def tile_oaclipv3_t_kernel(tc, img1, img2, W, b, out):
 
         raws, xgs, xcs, xss = {}, {}, {}, {}
         qs, qbs, trs, nrms, rns, rbcs, ngs, ncods, nscls = {}, {}, {}, {}, {}, {}, {}, {}, {}
-        rels, exs, rss, fins = {}, {}, {}, {}
+        rels, exs, rss, fins, rcs = {}, {}, {}, {}, {}
 
         def load_w(h):
             nc.sync.dma_start(out=w_raw[:, h], in_=W[h].rearrange("(p j) e -> p j e", j=PACK))
@@ -133,7 +132,7 @@ def tile_oaclipv3_t_kernel(tc, img1, img2, W, b, out):
                 qb = qbp.tile([P, PACK, NPOS], F32)
                 qbs[u] = qb
             bcol = b32[:, h * PACK + t : h * PACK + t + 1]
-            if t == 3 or (t == 1 and u < FILL):
+            if 1 <= u and (t == 3 or (1 <= t and u < FILL)):
                 nc.vector.tensor_scalar(
                     out=qbs[u][:, t, :], in0=qs[(u, t)][:], scalar1=bcol, scalar2=None, op0=ALU.add
                 )
@@ -255,14 +254,17 @@ def tile_oaclipv3_t_kernel(tc, img1, img2, W, b, out):
         def inv_colsum(u):
             i, h = divmod(u, H)
             cs = fins[u][:, L : L + 2 * MV_COLS].rearrange("p (m k) -> p m k", k=MV_COLS)
-            nc.vector.reciprocal(out=rcs[:, h, i, :, :], in_=cs[:, :, 0:2])
+            rc = smallp.tile([P, 2], F32)
+            nc.vector.reciprocal(out=rc[:], in_=cs[:, :, 0])
+            col12 = ((2 + h) * BS + i) * 2
+            nc.vector.tensor_copy(out=res[:, col12 : col12 + 2], in_=cs[:, :, 1])
+            rcs[u] = rc
 
         def spread_inv_colsum(u):
-            i, h = divmod(u, H)
             for mb in range(2):
                 nc.tensor.transpose(
                     out=fins[u][:, mb * P : (mb + 1) * P],
-                    in_=rcs[:, h, i, mb, 0:1].to_broadcast([P, P]),
+                    in_=rcs[u][:, mb : mb + 1].to_broadcast([P, P]),
                     identity=ident[:],
                 )
 
@@ -299,20 +301,20 @@ def tile_oaclipv3_t_kernel(tc, img1, img2, W, b, out):
             out=w_grp[:, 0].rearrange("p t m j -> p m j t"),
             in_=w_raw[:, 0].rearrange("p j (m t) -> p m j t", t=PACK),
         )
-        nc.scalar.copy(
-            out=w_grp[:, 1].rearrange("p t m j -> p m j t"),
-            in_=w_raw[:, 1].rearrange("p j (m t) -> p m j t", t=PACK),
-        )
+        nc.scalar.copy(out=b32[:], in_=b_raw[:].rearrange("p h t -> p (h t)"))
         regroup_img(0, 0)
         regroup_img(0, 1)
         load_img(RAW_BUFS)
         quant_w(0)
         quant_img(0)
-        nc.vector.tensor_copy(out=b32[:], in_=b_raw[:].rearrange("p h t -> p (h t)"))
+        nc.vector.tensor_copy(
+            out=w_grp[:, 1].rearrange("p t m j -> p m j t"),
+            in_=w_raw[:, 1].rearrange("p j (m t) -> p m j t", t=PACK),
+        )
+        quant_w(1)
         regroup_img(1, 0)
         regroup_img(1, 1)
         load_img(RAW_BUFS + 1)
-        quant_w(1)
 
         for k in range(-2, UNITS + 6):
             if live(k + 1):
@@ -375,10 +377,6 @@ def tile_oaclipv3_t_kernel(tc, img1, img2, W, b, out):
             if live(k - 4):
                 column_sums(k - 4)
 
-        nc.vector.reciprocal(
-            out=res[:, 64:128].rearrange("p (c f) -> p c f", f=2),
-            in_=rcs[:].rearrange("p h i m k -> p (h i) m k")[:, :, :, 1],
-        )
         resv = res[:].rearrange("p (c f) -> p c f", f=2)
         pair = const.tile([P, 128], F32)
         nc.vector.tensor_tensor(

from contextlib import ExitStack

import concourse.mybir as mybir
from concourse.masks import make_identity

FP8X4 = mybir.dt.float8_e4m3fn_x4
BF16 = mybir.dt.bfloat16
F32 = mybir.dt.float32
U32 = mybir.dt.uint32
U8 = mybir.dt.uint8
ALU = mybir.AluOpType
ACT = mybir.ActivationFunctionType

P = 128
BS, L, D, E, H = 16, 256, 512, 512, 2
PACK = 4
NPOS = 2 * L
UNITS = BS * H
LAMBDA = 10.0
FLOPS = 2 * (2 * BS * L) * D * (H * E) + 2 * H * BS * L * L * E
W2_SLOTS = 4
MV_COLS = 64
RAW_BUFS = 4
FILL = 5


def tile_oaclipv3_t_kernel(tc, img1, img2, W, b, out):
    nc = tc.nc
    with ExitStack() as ctx:
        const = ctx.enter_context(tc.tile_pool(name="const", bufs=1))
        rawp = ctx.enter_context(tc.tile_pool(name="rawp", bufs=RAW_BUFS))
        xgp = ctx.enter_context(tc.tile_pool(name="xgp", bufs=3))
        xcp = ctx.enter_context(tc.tile_pool(name="xcp", bufs=3))
        qbp = ctx.enter_context(tc.tile_pool(name="qbp", bufs=6))
        junkp = ctx.enter_context(tc.tile_pool(name="junkp", bufs=2))
        ngp = ctx.enter_context(tc.tile_pool(name="ngp", bufs=3))
        ncp = ctx.enter_context(tc.tile_pool(name="ncp", bufs=3))
        ep = ctx.enter_context(tc.tile_pool(name="ep", bufs=4))
        smallp = ctx.enter_context(tc.tile_pool(name="smallp", bufs=4))
        ring = ctx.enter_context(tc.psum_pool(name="ring", bufs=6))
        psr = ctx.enter_context(tc.psum_pool(name="psr", bufs=1))
        psfin = ctx.enter_context(tc.psum_pool(name="psfin", bufs=1))
        ctx.enter_context(tc.manual_schedule())

        w_raw = const.tile([P, H, PACK, E], BF16)
        b_raw = const.tile([P, H, PACK], BF16)
        ident = const.tile([P, P], F32)
        ones = const.tile([P, P], F32)
        mhalf = const.tile([P, 4], F32)
        w2 = const.tile([P, W2_SLOTS, 2, MV_COLS], F32)
        res = const.tile([P, 128], F32)
        b32 = const.tile([P, H * PACK], F32)
        w_grp = const.tile([P, H, PACK, P, PACK], BF16, align_bytes=64)
        w_cod = const.tile([P, H * PACK * P], U32, align_bytes=64)
        w_scl = const.tile([P, H * PACK * P], U8, align_bytes=64)

        raws, xgs, xcs, xss = {}, {}, {}, {}
        qs, qbs, trs, nrms, rns, rbcs, ngs, ncods, nscls = {}, {}, {}, {}, {}, {}, {}, {}, {}
        rels, exs, rss, fins, rcs = {}, {}, {}, {}, {}

        def load_w(h):
            nc.sync.dma_start(out=w_raw[:, h], in_=W[h].rearrange("(p j) e -> p j e", j=PACK))

        def load_img(i):
            raw = rawp.tile([P, 2, PACK, L], BF16)
            nc.sync.dma_start(out=raw[:, 0], in_=img1[i].rearrange("(p j) l -> p j l", j=PACK))
            nc.sync.dma_start(out=raw[:, 1], in_=img2[i].rearrange("(p j) l -> p j l", j=PACK))
            raws[i] = raw

        def quant_w(h):
            cols = slice(h * PACK * P, (h + 1) * PACK * P)
            nc.vector.quantize_mx(
                out=w_cod[:, cols].bitcast(FP8X4),
                scales=w_scl[:, cols],
                in_=w_grp[:, h].rearrange("p t m j -> p (t m j)"),
            )

        def gate_regroup(i, s):
            if s == 0:
                xg = xgp.tile([P, 2, L, PACK], BF16, align_bytes=64)
                xgs[i] = xg
            nc.vector.memset(xgs[i][:, s, 0:1, :], 0.0)

        def regroup_img(i, s):
            if i < 2:
                if s == 0:
                    xg = xgp.tile([P, 2, L, PACK], BF16, align_bytes=64)
                    xgs[i] = xg
                nc.vector.tensor_copy(
                    out=xgs[i][:, s].rearrange("p (c r) j -> p c j r", r=4),
                    in_=raws[i][:, s].rearrange("p j (c r) -> p c j r", r=4),
                )
            else:
                nc.gpsimd.tensor_scalar(
                    out=xgs[i][:, s],
                    in0=raws[i][:, s].rearrange("p j l -> p l j"),
                    scalar1=1.0,
                    scalar2=0.0,
                    op0=ALU.mult,
                    op1=ALU.add,
                )

        def quant_img(i):
            xc = xcp.tile([P, NPOS], U32, align_bytes=64)
            xs = xcp.tile([P, NPOS], U8, align_bytes=64)
            nc.vector.quantize_mx(
                out=xc[:].bitcast(FP8X4),
                scales=xs[:],
                in_=xgs[i][:].rearrange("p s l j -> p (s l j)"),
            )
            xcs[i] = xc
            xss[i] = xs

        def project(u, t):
            i, h = divmod(u, H)
            q = ring.tile([P, NPOS], F32, tag="feed")
            wcols = slice((h * PACK + t) * P, (h * PACK + t + 1) * P)
            nc.tensor.matmul_mx(
                out=q[:],
                lhsT=w_cod[:, wcols].bitcast(FP8X4),
                lhsT_scale=w_scl[:, wcols],
                rhs=xcs[i][:].bitcast(FP8X4),
                rhs_scale=xss[i][:],
                start=True,
                stop=True,
            )
            qs[(u, t)] = q

        def add_bias(u, t):
            h = u % H
            if t == 0:
                qb = qbp.tile([P, PACK, NPOS], F32)
                qbs[u] = qb
            bcol = b32[:, h * PACK + t : h * PACK + t + 1]
            if 1 <= u and (t == 3 or (1 <= t and u < FILL)):
                nc.vector.tensor_scalar(
                    out=qbs[u][:, t, :], in0=qs[(u, t)][:], scalar1=bcol, scalar2=None, op0=ALU.add
                )
            else:
                nc.scalar.activation(
                    out=qbs[u][:, t, :], in_=qs[(u, t)][:], func=ACT.Identity, bias=bcol, scale=1.0
                )

        def flip(u, c):
            tr = ring.tile([P, PACK * P], F32, tag="feed")
            for t in range(PACK):
                nc.tensor.transpose(
                    out=tr[:, t * P : (t + 1) * P],
                    in_=qbs[u][:, t, c * P : (c + 1) * P],
                    identity=ident[:],
                )
            trs[(u, c)] = tr

        def square_sum(u, c):
            if c == 0:
                nrm2 = smallp.tile([P, 4], F32)
                nrms[u] = nrm2
            sqj = junkp.tile([P, PACK * P], BF16)
            nc.scalar.activation(
                out=sqj[:], in_=trs[(u, c)][:], func=ACT.Square, accum_out=nrms[u][:, c : c + 1]
            )

        def inv_norm(u):
            ncl = smallp.tile([P, 4], F32)
            nc.gpsimd.tensor_scalar(
                out=ncl[:], in0=nrms[u][:], scalar1=1e-24, scalar2=None, op0=ALU.max
            )
            rn = smallp.tile([P, 4], F32)
            nc.gpsimd.tensor_tensor(out=rn[:], in0=ncl[:], in1=mhalf[:], op=ALU.pow)
            rns[u] = rn

        def spread_inv_norm(u):
            rbc = psr.tile([P, NPOS], F32)
            for c in range(4):
                nc.tensor.transpose(
                    out=rbc[:, c * P : (c + 1) * P],
                    in_=rns[u][:, c : c + 1].to_broadcast([P, P]),
                    identity=ident[:],
                )
            rbcs[u] = rbc

        def normalise(u):
            ng = ngp.tile([P, NPOS, PACK], BF16, align_bytes=64)
            nc.vector.tensor_tensor(
                out=ng[:].rearrange("p (c r) t -> p c t r", r=4),
                in0=qbs[u][:].rearrange("p t (c r) -> p c t r", r=4),
                in1=rbcs[u][:]
                .rearrange("p (c r) -> p c r", r=4)
                .unsqueeze(2)
                .to_broadcast([P, NPOS // 4, PACK, 4]),
                op=ALU.mult,
            )
            ngs[u] = ng

        def quant_n(u):
            ncod = ncp.tile([P, NPOS], U32, align_bytes=64)
            nscl = ncp.tile([P, NPOS], U8, align_bytes=64)
            nc.vector.quantize_mx(
                out=ncod[:].bitcast(FP8X4),
                scales=nscl[:],
                in_=ngs[u][:].rearrange("p c t -> p (c t)"),
            )
            ncods[u] = ncod
            nscls[u] = nscl

        def cosines(u):
            rel = ring.tile([P, 2, L], F32, tag="feed")
            for lb in range(2):
                nc.tensor.matmul_mx(
                    out=rel[:, lb, :],
                    lhsT=ncods[u][:, lb * P : (lb + 1) * P].bitcast(FP8X4),
                    lhsT_scale=nscls[u][:, lb * P : (lb + 1) * P],
                    rhs=ncods[u][:, L : 2 * L].bitcast(FP8X4),
                    rhs_scale=nscls[u][:, L : 2 * L],
                    start=True,
                    stop=True,
                )
            rels[u] = rel

        def exponent(u):
            ex = ep.tile([P, 2, L], F32)
            rs = smallp.tile([P, 2], F32)
            for lb in range(2):
                nc.scalar.activation(
                    out=ex[:, lb, :],
                    in_=rels[u][:, lb, :],
                    func=ACT.Exp,
                    bias=-LAMBDA,
                    scale=LAMBDA,
                    accum_out=rs[:, lb : lb + 1],
                )
            exs[u] = ex
            rss[u] = rs

        def inv_rowsum(u):
            nc.vector.reciprocal(out=w2[:, u % W2_SLOTS, :, 1], in_=rss[u][:])

        def column_sums(u):
            if u < UNITS - 2:
                fin = psfin.tile([P, 512], F32)
            else:
                fin = ring.tile([P, 512], F32, tag="feed")
            for mb in range(2):
                for lb in range(2):
                    nc.tensor.matmul(
                        out=fin[:, L + MV_COLS * mb : L + MV_COLS * (mb + 1)],
                        lhsT=exs[u][:, lb, mb * P : (mb + 1) * P],
                        rhs=w2[:, u % W2_SLOTS, lb, :],
                        start=(lb == 0),
                        stop=(lb == 1),
                    )
            fins[u] = fin

        def inv_colsum(u):
            i, h = divmod(u, H)
            cs = fins[u][:, L : L + 2 * MV_COLS].rearrange("p (m k) -> p m k", k=MV_COLS)
            rc = smallp.tile([P, 2], F32)
            nc.vector.reciprocal(out=rc[:], in_=cs[:, :, 0])
            col12 = ((2 + h) * BS + i) * 2
            nc.vector.tensor_copy(out=res[:, col12 : col12 + 2], in_=cs[:, :, 1])
            rcs[u] = rc

        def spread_inv_colsum(u):
            for mb in range(2):
                nc.tensor.transpose(
                    out=fins[u][:, mb * P : (mb + 1) * P],
                    in_=rcs[u][:, mb : mb + 1].to_broadcast([P, P]),
                    identity=ident[:],
                )

        def row_of_col_attn(u):
            i, h = divmod(u, H)
            col21 = (h * BS + i) * 2
            for lb in range(2):
                pj = junkp.tile([P, L], F32)
                nc.vector.scalar_tensor_tensor(
                    out=pj[:],
                    in0=exs[u][:, lb, :],
                    scalar=1.0,
                    in1=fins[u][:, 0:L],
                    op0=ALU.mult,
                    op1=ALU.mult,
                    accum_out=res[:, col21 + lb : col21 + lb + 1],
                )

        def live(u):
            return 0 <= u < UNITS

        load_w(0)
        load_img(0)
        load_w(1)
        for i in range(1, RAW_BUFS):
            load_img(i)
        with nc.allow_non_contiguous_dma(reason="bias: four neighbouring values to a partition"):
            nc.scalar.dma_start(out=b_raw[:], in_=b.rearrange("h (m t) -> m h t", t=PACK))
        make_identity(nc, ident[:])
        nc.vector.memset(mhalf[:], -0.5)
        nc.vector.memset(w2[:], 1.0)
        nc.vector.memset(ones[:], 1.0)
        nc.vector.tensor_copy(
            out=w_grp[:, 0].rearrange("p t m j -> p m j t"),
            in_=w_raw[:, 0].rearrange("p j (m t) -> p m j t", t=PACK),
        )
        nc.scalar.copy(out=b32[:], in_=b_raw[:].rearrange("p h t -> p (h t)"))
        regroup_img(0, 0)
        regroup_img(0, 1)
        load_img(RAW_BUFS)
        quant_w(0)
        quant_img(0)
        nc.vector.tensor_copy(
            out=w_grp[:, 1].rearrange("p t m j -> p m j t"),
            in_=w_raw[:, 1].rearrange("p j (m t) -> p m j t", t=PACK),
        )
        quant_w(1)
        regroup_img(1, 0)
        regroup_img(1, 1)
        load_img(RAW_BUFS + 1)

        for k in range(-2, UNITS + 6):
            if live(k + 1):
                project(k + 1, 0)
                project(k + 1, 1)
                add_bias(k + 1, 0)
            if live(k - 3):
                normalise(k - 3)
            if live(k + 1):
                add_bias(k + 1, 1)
            if live(k - 4):
                inv_rowsum(k - 4)
            if live(k):
                flip(k, 0)
            if live(k - 5):
                inv_colsum(k - 5)
            if live(k):
                flip(k, 1)
            if live(k + 1):
                project(k + 1, 2)
                project(k + 1, 3)
            if live(k):
                square_sum(k, 0)
            if live(k - 3):
                quant_n(k - 3)
            if k % 2 == 1 and 1 <= (k + 3) // 2 < BS:
                quant_img((k + 3) // 2)
            i = (k + 6) // 2 if k % 2 == 0 else (k + 5) // 2
            if 2 <= i < BS:
                gate_regroup(i, k % 2)
                regroup_img(i, k % 2)
                if k % 2 == 1 and i + RAW_BUFS < BS:
                    load_img(i + RAW_BUFS)
            if live(k - 5):
                spread_inv_colsum(k - 5)
            if live(k):
                flip(k, 2)
            if live(k + 1):
                add_bias(k + 1, 3)
            if live(k):
                square_sum(k, 1)
            if live(k - 2):
                spread_inv_norm(k - 2)
            if live(k):
                flip(k, 3)
            if live(k - 5):
                row_of_col_attn(k - 5)
            if live(k + 1):
                add_bias(k + 1, 2)
            if live(k):
                square_sum(k, 2)
            if live(k - 3):
                cosines(k - 3)
            if live(k):
                square_sum(k, 3)
            if live(k - 3):
                exponent(k - 3)
            if live(k):
                inv_norm(k)
            if live(k - 4):
                column_sums(k - 4)

        resv = res[:].rearrange("p (c f) -> p c f", f=2)
        pair = const.tile([P, 128], F32)
        nc.vector.tensor_tensor(
            out=pair[:].rearrange("p (c f) -> p c f", f=2),
            in0=resv[:, :, 0:1].to_broadcast([P, 64, 2]),
            in1=resv[:, :, 1:2].to_broadcast([P, 64, 2]),
            op=ALU.add,
        )
        rt = ring.tile([P, PACK * P], F32, tag="feed")
        nc.tensor.transpose(out=rt[:, 0:P], in_=res[:], identity=ident[:])
        nc.tensor.matmul(out=rt[:, P : P + 2], lhsT=pair[:], rhs=ones[:, 0:2], start=True, stop=True)
        den = const.tile([P, 1], F32)
        nc.vector.tensor_scalar(
            out=den[:], in0=rt[:, P : P + 1], scalar1=1e-8, scalar2=None, op0=ALU.add
        )
        rden = const.tile([P, 1], F32)
        nc.vector.reciprocal(out=rden[:], in_=den[:])
        o_sb = const.tile([P, P], F32)
        nc.vector.tensor_scalar(
            out=o_sb[:], in0=rt[:, 0:P], scalar1=rden[:, 0:1], scalar2=None, op0=ALU.mult
        )
        nc.sync.dma_start(out=out.rearrange("w h i (f p) -> (w h i f) p", p=P), in_=o_sb[:])
